import numpy as np
import ml_dtypes


def mxq(x, axis, fmt="e4m3"):
    dtype, down = {"e4m3": (ml_dtypes.float8_e4m3fn, 7), "e5m2": (ml_dtypes.float8_e5m2, 14)}[fmt]
    v = np.moveaxis(np.asarray(x, np.float32).astype(ml_dtypes.bfloat16).astype(np.float64), axis, -1)
    blocks = v.reshape(v.shape[:-1] + (-1, 32))
    amax = np.abs(blocks).max(-1, keepdims=True)
    byte = np.maximum(np.where(amax > 0, np.frexp(amax)[1] - 1 + 127, 0) - down, 1)
    scale = np.exp2(byte - 127.0)
    codes = (blocks / scale).astype(np.float32).astype(dtype).astype(np.float64)
    return np.moveaxis((codes * scale).reshape(v.shape), -1, axis)


WIDE = False


def mx_kscale(k):
    if not WIDE:
        return np.ones(k)
    levels = np.array([10, -10, 5, -5, 0])
    if k % 512:
        return np.exp2(np.random.permutation(np.resize(levels, k // 32))).repeat(32)
    a = np.empty((k // 512, 16))
    for p in range(k // 512):
        a[p, :8] = np.random.permutation(np.resize(levels, 8))
        for g in range(8):
            far = levels[np.abs(levels - a[p, g]) >= 10]
            a[p, g + 8] = far[np.random.randint(len(far))]
    return np.exp2(a.ravel()).repeat(32)


BF16 = ml_dtypes.bfloat16


def bf(x):
    return np.asarray(x, np.float32).astype(BF16)


def f64(x):
    return np.asarray(x).astype(np.float64)


E2M1 = np.array([0.0, 0.5, 1.0, 1.5, 2.0, 3.0, 4.0, 6.0, -0.0, -0.5, -1.0, -1.5, -2.0, -3.0, -4.0, -6.0])


def pack_weight(w, fmt):
    k, n = w.shape
    w = f64(bf(w)).reshape(k // 32, 32, n)
    amax = np.abs(w).max(1)
    if fmt == "e4m3":
        byte = np.frexp(amax)[1] - 1 + 127 - 7
    else:
        mant, ex = np.frexp(amax / 6.0)
        byte = np.where(mant > 0.5, ex, ex - 1) + 127
    byte = np.clip(np.where(amax > 0, byte, 1), 1, 254)
    scaled = (w * np.exp2(127.0 - byte)[:, None, :]).reshape(k, n).astype(np.float32)
    by_word = np.ascontiguousarray(scaled.reshape(k // 512, 128, 4, n).transpose(0, 1, 3, 2))
    if fmt == "e4m3":
        words = by_word.astype(ml_dtypes.float8_e4m3fn).view(np.uint8)
    else:
        c = by_word.astype(ml_dtypes.float4_e2m1fn).view(np.uint8) & 0xF
        words = c[..., 0::2] | (c[..., 1::2] << 4)
    return np.ascontiguousarray(words), np.ascontiguousarray(byte.astype(np.uint8).reshape(k // 512, 16, n))


def unpack_weight(words, scales, fmt):
    g, p, n, _ = words.shape
    if fmt == "e4m3":
        vals = np.ascontiguousarray(words).view(ml_dtypes.float8_e4m3fn).astype(np.float64)
    else:
        nib = np.empty((g, p, n, 4), np.uint8)
        nib[..., 0::2] = words & 0xF
        nib[..., 1::2] = words >> 4
        vals = E2M1[nib]
    vals = vals * np.repeat(np.exp2(scales.astype(np.float64) - 127.0), 8, axis=1)[..., None]
    return vals.transpose(0, 1, 3, 2).reshape(g * 512, n)
def pack4(w):
    words, scales = pack_weight(w, "e2m1")
    return words.reshape(words.shape[0], 128, -1), scales


def unpack4(words, scales):
    return unpack_weight(words.reshape(words.shape[0], 128, -1, 2), scales, "e2m1")


B, S, D, N, A, F = 64, 64, 512, 128, 128, 512


def draw0():
    s, t, u = mx_kscale(D), mx_kscale(F), mx_kscale(F)
    slots = bf(np.random.standard_normal((B, S, D)) * s)
    ident = bf(np.random.standard_normal((N, F)) * t)
    Wq = np.random.standard_normal((F, D)) / np.sqrt(D) / s[None, :] * u[:, None]
    Wk = np.random.standard_normal((F, F)) * 2.0 / np.sqrt(F) / t[None, :] / u[:, None]
    Wq_words, Wq_scales = pack4(Wq.T)
    Wk_words, Wk_scales = pack4(Wk.T)
    return {
        "slots": slots,
        "ident": ident,
        "Wq_words": Wq_words,
        "Wq_scales": Wq_scales,
        "Wk_words": Wk_words,
        "Wk_scales": Wk_scales,
    }


def core(slots, ident, Wq_words, Wq_scales, Wk_words, Wk_scales):
    q = mxq(f64(slots), 2, "e4m3") @ unpack4(Wq_words, Wq_scales)
    k = mxq(f64(ident), 1, "e4m3") @ unpack4(Wk_words, Wk_scales)
    logits = D ** (-0.5) * (mxq(k, 1, "e4m3") @ mxq(q, 2, "e4m3").transpose(0, 2, 1))
    e = np.exp(logits - logits.max(-1, keepdims=True))
    return e / e.sum(-1, keepdims=True)


def e4m3fn_bytes(y):
    return np.clip(np.asarray(y, np.float64), -448.0, 448.0).astype(np.float32).astype(ml_dtypes.float8_e4m3fn).view(np.uint8)


def e4m3fn_values(b):
    return np.asarray(b, np.uint8).view(ml_dtypes.float8_e4m3fn).astype(np.float64)


def setup_inputs():
    d = draw0()
    x0 = np.asarray(d['slots']).astype(np.float64)
    s = (np.max(np.abs(x0), axis=(0, 1), keepdims=True) / 448.0).astype(np.float32)
    out = {}
    for k, v in d.items():
        if k == 'slots':
            out['slots_bytes'] = e4m3fn_bytes(x0 / s.astype(np.float64))
            out['slots_scale'] = s
        else:
            out[k] = v
    return out


def reference(slots_bytes, slots_scale, ident, Wq_words, Wq_scales, Wk_words, Wk_scales):
    return core(e4m3fn_values(slots_bytes) * slots_scale.astype(np.float64), ident, Wq_words, Wq_scales, Wk_words, Wk_scales)

@@ -1,0 +1,342 @@
+from contextlib import ExitStack
+
+import concourse.mybir as mybir
+from concourse.masks import make_identity
+
+F32 = mybir.dt.float32
+BF16 = mybir.dt.bfloat16
+I32 = mybir.dt.int32
+U32 = mybir.dt.uint32
+U8 = mybir.dt.uint8
+FP8 = mybir.dt.float8_e4m3fn
+FP8X4 = mybir.dt.float8_e4m3fn_x4
+FP4X4 = mybir.dt.float4_e2m1fn_x4
+MULT = mybir.AluOpType.mult
+MAX = mybir.AluOpType.max
+AXIS_X = mybir.AxisListType.X
+EXP = mybir.ActivationFunctionType.Exp
+
+B, S, D, N, F = 64, 64, 512, 128, 512
+P = 128
+FLOPS = 2 * B * S * D * F + 2 * N * F * F + 2 * B * N * S * F
+
+ROWS = B * S
+PAIRS = ROWS // (2 * P)
+CHUNKS = PAIRS // 2
+CB = 512 // S
+LOGIT_SCALE = float(D) ** -0.5
+
+
+def tile_actionbindingattention_pb_w4_kernel(
+    tc, slots_bytes, slots_scale, ident, Wq_words, Wq_scales, Wk_words, Wk_scales, out
+):
+    nc = tc.nc
+    with ExitStack() as ctx:
+        const = ctx.enter_context(tc.tile_pool(name="const", bufs=1))
+        work = ctx.enter_context(tc.tile_pool(name="work", bufs=4))
+        outs = ctx.enter_context(tc.tile_pool(name="outs", bufs=11))
+        psx = ctx.enter_context(tc.psum_pool(name="psx", bufs=2))
+        psq = ctx.enter_context(tc.psum_pool(name="psq", bufs=4))
+        psl = ctx.enter_context(tc.psum_pool(name="psl", bufs=2))
+        ctx.enter_context(tc.manual_schedule())
+
+        xb = []
+        rows_flat = slots_bytes.rearrange("b s k -> (b s) k")
+
+        def load_x(first, count):
+            t = const.tile([P, 2 * count, D], U8, name="xb%d" % first, align_bytes=64)
+            src = rows_flat[first * 2 * P : (first + count) * 2 * P, :]
+            nc.sync.dma_start(out=t[:], in_=src.rearrange("(j p) k -> p j k", p=P))
+            for i in range(count):
+                xb.append(t[:, 2 * i : 2 * i + 2, :])
+
+        s_bc = const.tile([P, 2, D], F32, name="s_bc", align_bytes=64)
+        nc.scalar.dma_start(
+            out=s_bc[:, 0, :], in_=slots_scale.rearrange("a b k -> (a b k)").partition_broadcast(P)
+        )
+        load_x(0, 1)
+        idb = const.tile([P, F], BF16, name="idb", align_bytes=64)
+        nc.scalar.dma_start(out=idb[:], in_=ident)
+        warm = const.tile([P, 1], F32, name="warm")
+        nc.vector.memset(warm[:], 0.0)
+        nc.scalar.activation(out=warm[:], in_=warm[:], func=EXP)
+
+        identf = const.tile([P, P], F32, name="identf", align_bytes=64)
+        make_identity(nc, identf[:])
+        ws_raw = const.tile([P, 2, F], U8, name="ws_raw", align_bytes=64)
+        nc.vector.memset(ws_raw[:].rearrange("p w n -> p (w n)").bitcast(I32), 0)
+        ww_raw = const.tile([P, 2, 2 * F], U8, name="ww_raw", align_bytes=64)
+        ww = const.tile([P, 2, 2 * F], U8, name="ww", align_bytes=64)
+        ws = const.tile([P, 2, F], U8, name="ws", align_bytes=64)
+
+        def load_w(w, words, scales):
+            nc.sync.dma_start(out=ww_raw[:, w, :].bitcast(I32), in_=words[0].bitcast(I32))
+            for q in range(4):
+                nc.sync.dma_start(
+                    out=ws_raw[32 * q : 32 * q + 4, w, :].bitcast(I32),
+                    in_=scales[0, 4 * q : 4 * q + 4, :].bitcast(I32),
+                )
+
+        def permute_words(eng, w):
+            eng.tensor_copy(
+                out=ww[:, w, :].bitcast(I32).rearrange("p (t g e) -> p t g e", t=4, e=2),
+                in_=ww_raw[:, w, :].bitcast(I32).rearrange("p (g t e) -> p t g e", t=4, e=2),
+            )
+
+        def permute_scales(eng, w):
+            eng.tensor_copy(
+                out=ws[:, w, :].bitcast(I32).rearrange("p (t g) -> p t g", t=4),
+                in_=ws_raw[:, w, :].bitcast(I32).rearrange("p (g t) -> p t g", t=4),
+            )
+
+        load_w(0, Wq_words, Wq_scales)
+        load_x(1, 1)
+        load_w(1, Wk_words, Wk_scales)
+        for first in range(2, PAIRS, 2):
+            load_x(first, 2)
+
+        xs, xt, xg, xq, qp, qg, qq, lg = {}, {}, {}, {}, {}, {}, {}, {}
+        nb, ex, sm = {}, {}, {}
+        units = [(4 * c, 4) for c in range(CHUNKS - 1)] + [(28, 2), (30, 1), (31, 1)]
+
+        def stage_a(i):
+            t = work.tile([P, 2, D], BF16, name="xs", align_bytes=64)
+            if i < 2:
+                for j in range(2):
+                    nc.vector.tensor_tensor(
+                        out=t[:, j, :], in0=xb[i][:, j, :].bitcast(FP8), in1=s_bc[:, 0, :], op=MULT
+                    )
+            else:
+                nc.vector.tensor_tensor(
+                    out=t[:].rearrange("p j k -> p (j k)"),
+                    in0=xb[i].rearrange("p j k -> p (j k)").bitcast(FP8),
+                    in1=s_bc[:].rearrange("p j k -> p (j k)"),
+                    op=MULT,
+                )
+            xs[i] = t
+
+        def transposes(src, dst):
+            words = src.bitcast(F32)
+            for u in range(2):
+                nc.tensor.transpose(dst[:, u, :], words[:, u::2], identf[:])
+
+        def stage_t(i):
+            t = psx.tile([P, 2, 2, P], F32, name="xt")
+            for j in range(2):
+                transposes(xs[i][:, j, :], t[:, j])
+            xt[i] = t
+
+        def head_pair():
+            t = work.tile([P, 2, P, 4], BF16, name="xg", align_bytes=64)
+            for j in range(2):
+                h = psx.tile([P, 2, P], F32, name="xt")
+                transposes(xs[0][:, j, :], h)
+                nc.scalar.copy(
+                    out=t[:, j].rearrange("p r t -> p (r t)").bitcast(F32).rearrange("p (r u) -> p r u", u=2),
+                    in_=h[:].rearrange("p u r -> p r u"),
+                )
+            xg[0] = t
+
+        def stage_b(i, parts=1):
+            t = work.tile([P, 2, P, 4], BF16, name="xg", align_bytes=64)
+            n = 2 // parts
+            for h in range(parts):
+                js = slice(n * h, n * h + n)
+                nc.scalar.copy(
+                    out=t[:, js].rearrange("p j r t -> p j (r t)").bitcast(F32).rearrange("p j (r u) -> p j r u", u=2),
+                    in_=xt[i][:, js].rearrange("p j u r -> p j r u"),
+                )
+            xg[i] = t
+
+        def stage_q1(i, parts=1):
+            c = work.tile([P, 2 * P], U32, name="xq", align_bytes=64)
+            s = work.tile([P, 2 * P], U8, name="xqs", align_bytes=64)
+            n = 2 // parts
+            for h in range(parts):
+                cols = slice(P * n * h, P * n * (h + 1))
+                nc.vector.quantize_mx(
+                    out=c[:, cols].bitcast(FP8X4),
+                    scales=s[:, cols],
+                    in_=xg[i][:, n * h : n * h + n].rearrange("p j r t -> p (j r t)"),
+                )
+            xq[i] = (c, s)
+
+        def project(w, codes, scales):
+            t = psq.tile([P, 4, P], F32, name="qp")
+            for f in range(4):
+                nc.tensor.matmul_mx(
+                    out=t[:, f, :],
+                    lhsT=ww[:, w, 2 * P * f : 2 * P * (f + 1)].bitcast(FP4X4),
+                    lhsT_scale=ws[:, w, P * f : P * (f + 1)],
+                    rhs=codes.bitcast(FP8X4),
+                    rhs_scale=scales,
+                    start=True,
+                    stop=True,
+                )
+            return t
+
+        def stage_m1(i):
+            c, s = xq[i]
+            qp[i] = [project(0, c[:, P * j : P * (j + 1)], s[:, P * j : P * (j + 1)]) for j in range(2)]
+
+        def stage_d(i, last=False):
+            t = work.tile([P, 2, P, 4], BF16, name="qg", align_bytes=64)
+            for j in range(2):
+                src = qp[i][j][:].rearrange("p t r -> p r t")
+                if last and j == 1:
+                    nc.vector.tensor_copy(out=t[:, j], in_=src)
+                else:
+                    nc.scalar.copy(out=t[:, j], in_=src)
+            qg[i] = t
+
+        def stage_q2(i, parts=1):
+            h = i % 2
+            if h == 0:
+                c = work.tile([P, 4 * P], U32, name="qq", align_bytes=64)
+                s = work.tile([P, 4 * P], U8, name="qqs", align_bytes=64)
+                qq[i // 2] = (c, s)
+            c, s = qq[i // 2]
+            n = 2 // parts
+            for g in range(parts):
+                cols = slice(P * (2 * h + n * g), P * (2 * h + n * g + n))
+                nc.vector.quantize_mx(
+                    out=c[:, cols].bitcast(FP8X4),
+                    scales=s[:, cols],
+                    in_=qg[i][:, n * g : n * g + n].rearrange("p j r t -> p (j r t)"),
+                )
+
+        def stage_m2(c):
+            first, tiles = units[c]
+            if tiles == 1:
+                t = psx.tile([P, 2, S], F32, name="xt")
+            else:
+                t = psl.tile([P, 2 * tiles, S], F32, name="lg")
+            codes, scales = qq[first // 4]
+            cols = slice(P * (first % 4), P * (first % 4 + tiles))
+            nc.tensor.matmul_mx(
+                out=t[:].rearrange("p b s -> p (b s)"),
+                lhsT=kq[:].bitcast(FP8X4),
+                lhsT_scale=kqs[:],
+                rhs=codes[:, cols].bitcast(FP8X4),
+                rhs_scale=scales[:, cols],
+                start=True,
+                stop=True,
+            )
+            lg[c] = t
+
+        def stage_max(c):
+            samples = 2 * units[c][1]
+            mx = work.tile([P, samples], F32, name="mx")
+            nc.vector.tensor_reduce(out=mx[:], in_=lg[c][:], axis=AXIS_X, op=MAX)
+            t = work.tile([P, samples], F32, name="nb")
+            eng = nc.gpsimd if samples == CB else nc.vector
+            eng.tensor_scalar(out=t[:], in0=mx[:], scalar1=-LOGIT_SCALE, scalar2=None, op0=MULT)
+            nb[c] = t
+            ex[c] = work.tile([P, samples, S], F32, name="ex")
+            sm[c] = work.tile([P, samples], F32, name="sm")
+
+        def stage_exp(c, samples):
+            for b in samples:
+                nc.scalar.activation(
+                    out=ex[c][:, b, :],
+                    in_=lg[c][:, b, :],
+                    func=EXP,
+                    bias=nb[c][:, b : b + 1],
+                    scale=LOGIT_SCALE,
+                    accum_out=sm[c][:, b : b + 1],
+                )
+
+        def stage_mul(c):
+            first, tiles = units[c]
+            samples = 2 * tiles
+            rc = work.tile([P, samples], F32, name="rc")
+            nc.vector.reciprocal(out=rc[:], in_=sm[c][:])
+            o = outs.tile([P, samples, S], F32, name="o")
+            nc.vector.tensor_tensor(
+                out=o[:], in0=ex[c][:], in1=rc[:].unsqueeze(2).to_broadcast([P, samples, S]), op=MULT
+            )
+            nc.sync.dma_start(
+                out=out[2 * first : 2 * first + samples].rearrange("b n s -> n b s"), in_=o[:]
+            )
+
+        ig = const.tile([P, P, 4], BF16, name="ig", align_bytes=64)
+        iq = const.tile([P, P], U32, name="iq", align_bytes=64)
+        iqs = const.tile([P, P], U8, name="iqs", align_bytes=64)
+        kg = const.tile([P, P, 4], BF16, name="kg", align_bytes=64)
+        kq = const.tile([P, P], U32, name="kq", align_bytes=64)
+        kqs = const.tile([P, P], U8, name="kqs", align_bytes=64)
+        it = psl.tile([P, 2, P], F32, name="lg")
+        transposes(idb[:], it)
+        nc.scalar.copy(
+            out=ig[:].rearrange("p r t -> p (r t)").bitcast(F32).rearrange("p (r u) -> p r u", u=2),
+            in_=it[:].rearrange("p u r -> p r u"),
+        )
+        stage_a(0)
+        head_pair()
+        permute_words(nc.vector, 0)
+        permute_scales(nc.gpsimd, 0)
+        nc.gpsimd.tensor_copy(out=s_bc[:, 1, :], in_=s_bc[:, 0, :])
+        stage_q1(0, 2)
+        stage_m1(0)
+        permute_words(nc.gpsimd, 1)
+        permute_scales(nc.gpsimd, 1)
+        stage_a(1)
+        stage_t(1)
+        nc.vector.quantize_mx(out=iq[:].bitcast(FP8X4), scales=iqs[:], in_=ig[:].rearrange("p r t -> p (r t)"))
+        stage_d(0)
+        stage_b(1)
+        stage_a(2)
+
+        for i in range(1, PAIRS - 1):
+            if i + 2 < PAIRS:
+                stage_a(i + 2)
+            stage_t(i + 1)
+            if i > 1:
+                stage_d(i - 1)
+            if i == 2:
+                nc.scalar.copy(out=kg[:], in_=kp[:].rearrange("p t r -> p r t"))
+            stage_q1(i)
+            stage_m1(i)
+            if i == 1:
+                kp = project(1, iq[:], iqs[:])
+            stage_q2(i - 1)
+            if i == 2:
+                nc.vector.quantize_mx(
+                    out=kq[:].bitcast(FP8X4), scales=kqs[:], in_=kg[:].rearrange("p r t -> p (r t)")
+                )
+            if i % 2 == 0:
+                stage_m2(i // 2 - 1)
+                if 4 <= i:
+                    stage_exp(i // 2 - 2, range(4))
+                if 6 <= i:
+                    stage_mul(i // 2 - 3)
+            else:
+                if 3 <= i:
+                    stage_max((i - 3) // 2)
+                if 5 <= i:
+                    stage_exp((i - 5) // 2, range(4, 8))
+            stage_b(i + 1)
+
+        stage_d(14)
+        stage_q1(15)
+        stage_m1(15)
+        stage_max(6)
+        stage_exp(5, range(4, 8))
+        stage_d(15, last=True)
+        stage_q2(14)
+        stage_m2(7)
+        stage_exp(6, range(8))
+        stage_q2(15, 2)
+        stage_m2(8)
+        stage_m2(9)
+        stage_max(7)
+        stage_mul(5)
+        stage_max(8)
+        stage_max(9)
+        stage_exp(7, range(4))
+        stage_mul(6)
+        stage_exp(8, range(2))
+        stage_exp(9, range(2))
+        stage_mul(7)
+        stage_mul(8)
+        stage_mul(9)

@@ -50,11 +50,9 @@ def tile_actionbindingattention_pb_w4_kernel(
             for i in range(count):
                 xb.append(t[:, 2 * i : 2 * i + 2, :])
 
+        s4 = const.tile([P, 4], F32, name="s4")
+        nc.scalar.dma_start(out=s4[:], in_=slots_scale.rearrange("a b (p t) -> p (a b t)", t=4))
         s_bc = const.tile([P, 2, D], F32, name="s_bc", align_bytes=64)
-        nc.scalar.dma_start(
-            out=s_bc[:, 0, :], in_=slots_scale.rearrange("a b k -> (a b k)").partition_broadcast(P)
-        )
-        load_x(0, 1)
         idb = const.tile([P, F], BF16, name="idb", align_bytes=64)
         nc.scalar.dma_start(out=idb[:], in_=ident)
         warm = const.tile([P, 1], F32, name="warm")
@@ -90,6 +88,7 @@ def tile_actionbindingattention_pb_w4_kernel(
             )
 
         load_w(0, Wq_words, Wq_scales)
+        load_x(0, 1)
         load_x(1, 1)
         load_w(1, Wk_words, Wk_scales)
         for first in range(2, PAIRS, 2):
@@ -229,8 +228,7 @@ def tile_actionbindingattention_pb_w4_kernel(
             mx = work.tile([P, samples], F32, name="mx")
             nc.vector.tensor_reduce(out=mx[:], in_=lg[c][:], axis=AXIS_X, op=MAX)
             t = work.tile([P, samples], F32, name="nb")
-            eng = nc.gpsimd if samples == CB else nc.vector
-            eng.tensor_scalar(out=t[:], in0=mx[:], scalar1=-LOGIT_SCALE, scalar2=None, op0=MULT)
+            nc.vector.tensor_scalar(out=t[:], in0=mx[:], scalar1=-LOGIT_SCALE, scalar2=None, op0=MULT)
             nb[c] = t
             ex[c] = work.tile([P, samples, S], F32, name="ex")
             sm[c] = work.tile([P, samples], F32, name="sm")
@@ -265,6 +263,15 @@ def tile_actionbindingattention_pb_w4_kernel(
         kg = const.tile([P, P, 4], BF16, name="kg", align_bytes=64)
         kq = const.tile([P, P], U32, name="kq", align_bytes=64)
         kqs = const.tile([P, P], U8, name="kqs", align_bytes=64)
+        sp = psl.tile([P, 4, P], F32, name="lg")
+        for t in range(4):
+            nc.tensor.transpose(sp[:, t, :], s4[:, t : t + 1].to_broadcast([P, P]), identf[:])
+        for j in range(2):
+            nc.scalar.copy(
+                out=s_bc[:, j, :].rearrange("p (n t) -> p n t", t=4), in_=sp[:].rearrange("p t n -> p n t")
+            )
+        permute_words(nc.vector, 0)
+        permute_scales(nc.vector, 0)
         it = psl.tile([P, 2, P], F32, name="lg")
         transposes(idb[:], it)
         nc.scalar.copy(
@@ -273,15 +280,12 @@ def tile_actionbindingattention_pb_w4_kernel(
         )
         stage_a(0)
         head_pair()
-        permute_words(nc.vector, 0)
-        permute_scales(nc.gpsimd, 0)
-        nc.gpsimd.tensor_copy(out=s_bc[:, 1, :], in_=s_bc[:, 0, :])
         stage_q1(0, 2)
         stage_m1(0)
-        permute_words(nc.gpsimd, 1)
-        permute_scales(nc.gpsimd, 1)
         stage_a(1)
         stage_t(1)
+        permute_words(nc.vector, 1)
+        permute_scales(nc.vector, 1)
         nc.vector.quantize_mx(out=iq[:].bitcast(FP8X4), scales=iqs[:], in_=ig[:].rearrange("p r t -> p (r t)"))
         stage_d(0)
         stage_b(1)

@@ -14,6 +14,7 @@ FP4X4 = mybir.dt.float4_e2m1fn_x4
 MULT = mybir.AluOpType.mult
 MAX = mybir.AluOpType.max
 AXIS_X = mybir.AxisListType.X
+COPY = mybir.ActivationFunctionType.Copy
 EXP = mybir.ActivationFunctionType.Exp
 
 B, S, D, N, F = 64, 64, 512, 128, 512
@@ -87,15 +88,15 @@ def tile_actionbindingattention_pb_w4_kernel(
                 in_=ws_raw[:, w, :].bitcast(I32).rearrange("p (g t) -> p t g", t=4),
             )
 
-        load_w(0, Wq_words, Wq_scales)
         load_x(0, 1)
+        load_w(0, Wq_words, Wq_scales)
         load_x(1, 1)
         load_w(1, Wk_words, Wk_scales)
         for first in range(2, PAIRS, 2):
             load_x(first, 2)
 
         xs, xt, xg, xq, qp, qg, qq, lg = {}, {}, {}, {}, {}, {}, {}, {}
-        nb, ex, sm = {}, {}, {}
+        top, nb, ex, sm, rcp = {}, {}, {}, {}, {}
         units = [(4 * c, 4) for c in range(CHUNKS - 1)] + [(28, 2), (30, 1), (31, 1)]
 
         def stage_a(i):
@@ -160,8 +161,12 @@ def tile_actionbindingattention_pb_w4_kernel(
                 )
             xq[i] = (c, s)
 
-        def project(w, codes, scales):
+        def project(w, codes, scales, fill=False):
             t = psq.tile([P, 4, P], F32, name="qp")
+            if fill:
+                nc.tensor.matmul(
+                    t[:].rearrange("p t r -> p (t r)"), lhsT=idb[:, :P], rhs=idb[:], start=True, stop=True
+                )
             for f in range(4):
                 nc.tensor.matmul_mx(
                     out=t[:, f, :],
@@ -174,40 +179,36 @@ def tile_actionbindingattention_pb_w4_kernel(
                 )
             return t
 
-        def stage_m1(i):
+        def stage_m1(i, fill=True):
             c, s = xq[i]
-            qp[i] = [project(0, c[:, P * j : P * (j + 1)], s[:, P * j : P * (j + 1)]) for j in range(2)]
+            qp[i] = [project(0, c[:, P * j : P * (j + 1)], s[:, P * j : P * (j + 1)], fill and j == 0) for j in range(2)]
 
-        def stage_d(i, last=False):
-            t = work.tile([P, 2, P, 4], BF16, name="qg", align_bytes=64)
+        def stage_d(i, copies=(nc.scalar.copy, nc.scalar.copy)):
+            if i not in qg:
+                qg[i] = work.tile([P, 2, P, 4], BF16, name="qg", align_bytes=64)
             for j in range(2):
-                src = qp[i][j][:].rearrange("p t r -> p r t")
-                if last and j == 1:
-                    nc.vector.tensor_copy(out=t[:, j], in_=src)
-                else:
-                    nc.scalar.copy(out=t[:, j], in_=src)
-            qg[i] = t
+                if copies[j]:
+                    copies[j](out=qg[i][:, j], in_=qp[i][j][:].rearrange("p t r -> p r t"))
 
-        def stage_q2(i, parts=1):
+        def stage_q2(i, tiles=None):
             h = i % 2
-            if h == 0:
+            if i // 2 not in qq:
                 c = work.tile([P, 4 * P], U32, name="qq", align_bytes=64)
                 s = work.tile([P, 4 * P], U8, name="qqs", align_bytes=64)
                 qq[i // 2] = (c, s)
             c, s = qq[i // 2]
-            n = 2 // parts
-            for g in range(parts):
-                cols = slice(P * (2 * h + n * g), P * (2 * h + n * g + n))
-                nc.vector.quantize_mx(
-                    out=c[:, cols].bitcast(FP8X4),
-                    scales=s[:, cols],
-                    in_=qg[i][:, n * g : n * g + n].rearrange("p j r t -> p (j r t)"),
-                )
+            lo, hi = (tiles[0], tiles[0] + 1) if tiles else (0, 2)
+            cols = slice(P * (2 * h + lo), P * (2 * h + hi))
+            nc.vector.quantize_mx(
+                out=c[:, cols].bitcast(FP8X4),
+                scales=s[:, cols],
+                in_=qg[i][:, lo:hi].rearrange("p j r t -> p (j r t)"),
+            )
 
         def stage_m2(c):
             first, tiles = units[c]
-            if tiles == 1:
-                t = psx.tile([P, 2, S], F32, name="xt")
+            if c in (7, 8):
+                t = psx.tile([P, 2 * tiles, S], F32, name="xt")
             else:
                 t = psl.tile([P, 2 * tiles, S], F32, name="lg")
             codes, scales = qq[first // 4]
@@ -225,13 +226,17 @@ def tile_actionbindingattention_pb_w4_kernel(
 
         def stage_max(c):
             samples = 2 * units[c][1]
-            mx = work.tile([P, samples], F32, name="mx")
+            mx = outs.tile([P, samples], F32, name="mx")
             nc.vector.tensor_reduce(out=mx[:], in_=lg[c][:], axis=AXIS_X, op=MAX)
-            t = work.tile([P, samples], F32, name="nb")
-            nc.vector.tensor_scalar(out=t[:], in0=mx[:], scalar1=-LOGIT_SCALE, scalar2=None, op0=MULT)
+            top[c] = mx
+
+        def stage_nb(c):
+            samples = 2 * units[c][1]
+            t = outs.tile([P, samples], F32, name="nb")
+            nc.vector.tensor_scalar(out=t[:], in0=top[c][:], scalar1=-LOGIT_SCALE, scalar2=None, op0=MULT)
             nb[c] = t
-            ex[c] = work.tile([P, samples, S], F32, name="ex")
-            sm[c] = work.tile([P, samples], F32, name="sm")
+            ex[c] = outs.tile([P, samples, S], F32, name="ex")
+            sm[c] = outs.tile([P, samples], F32, name="sm")
 
         def stage_exp(c, samples):
             for b in samples:
@@ -244,15 +249,41 @@ def tile_actionbindingattention_pb_w4_kernel(
                     accum_out=sm[c][:, b : b + 1],
                 )
 
+        def stage_rc(c):
+            rcp[c] = outs.tile([P, 2 * units[c][1]], F32, name="rc")
+            nc.vector.reciprocal(out=rcp[c][:], in_=sm[c][:])
+
         def stage_mul(c):
             first, tiles = units[c]
             samples = 2 * tiles
-            rc = work.tile([P, samples], F32, name="rc")
-            nc.vector.reciprocal(out=rc[:], in_=sm[c][:])
+            rc = rcp[c]
             o = outs.tile([P, samples, S], F32, name="o")
             nc.vector.tensor_tensor(
                 out=o[:], in0=ex[c][:], in1=rc[:].unsqueeze(2).to_broadcast([P, samples, S]), op=MULT
             )
+            nc.sync.dma_start(
+                out=out[2 * first : 2 * first + samples].rearrange("b n s -> n b s"), in_=o[:]
+            )
+
+        def stage_mul_gpsimd(c):
+            first, tiles = units[c]
+            samples = 2 * tiles
+            o = outs.tile([P, samples, S], F32, name="o")
+            nc.gpsimd.tensor_tensor(
+                out=o[:], in0=ex[c][:], in1=rcp[c][:].unsqueeze(2).to_broadcast([P, samples, S]), op=MULT
+            )
+            nc.sync.dma_start(
+                out=out[2 * first : 2 * first + samples].rearrange("b n s -> n b s"), in_=o[:]
+            )
+
+        def stage_mul_scalar(c):
+            first, tiles = units[c]
+            samples = 2 * tiles
+            o = outs.tile([P, samples, S], F32, name="o")
+            for b in range(samples):
+                nc.scalar.activation(
+                    out=o[:, b, :], in_=ex[c][:, b, :], func=COPY, scale=rcp[c][:, b : b + 1]
+                )
             nc.sync.dma_start(
                 out=out[2 * first : 2 * first + samples].rearrange("b n s -> n b s"), in_=o[:]
             )
@@ -270,8 +301,6 @@ def tile_actionbindingattention_pb_w4_kernel(
             nc.scalar.copy(
                 out=s_bc[:, j, :].rearrange("p (n t) -> p n t", t=4), in_=sp[:].rearrange("p t n -> p n t")
             )
-        permute_words(nc.vector, 0)
-        permute_scales(nc.vector, 0)
         it = psl.tile([P, 2, P], F32, name="lg")
         transposes(idb[:], it)
         nc.scalar.copy(
@@ -280,6 +309,8 @@ def tile_actionbindingattention_pb_w4_kernel(
         )
         stage_a(0)
         head_pair()
+        permute_words(nc.vector, 0)
+        permute_scales(nc.vector, 0)
         stage_q1(0, 2)
         stage_m1(0)
         stage_a(1)
@@ -292,10 +323,14 @@ def tile_actionbindingattention_pb_w4_kernel(
         stage_a(2)
 
         for i in range(1, PAIRS - 1):
+            if i % 2 == 0 and i >= 6:
+                stage_rc(i // 2 - 3)
             if i + 2 < PAIRS:
                 stage_a(i + 2)
             stage_t(i + 1)
-            if i > 1:
+            if i == PAIRS - 2:
+                stage_d(i - 1, (nc.scalar.copy, None))
+            elif i > 1:
                 stage_d(i - 1)
             if i == 2:
                 nc.scalar.copy(out=kg[:], in_=kp[:].rearrange("p t r -> p r t"))
@@ -303,6 +338,10 @@ def tile_actionbindingattention_pb_w4_kernel(
             stage_m1(i)
             if i == 1:
                 kp = project(1, iq[:], iqs[:])
+            if i == PAIRS - 2:
+                stage_d(i - 1, (None, nc.vector.tensor_copy))
+            if i % 2 == 1 and i >= 3:
+                stage_max((i - 3) // 2)
             stage_q2(i - 1)
             if i == 2:
                 nc.vector.quantize_mx(
@@ -310,37 +349,48 @@ def tile_actionbindingattention_pb_w4_kernel(
                 )
             if i % 2 == 0:
                 stage_m2(i // 2 - 1)
-                if 4 <= i:
+                if i >= 4:
                     stage_exp(i // 2 - 2, range(4))
-                if 6 <= i:
+                if i >= 6:
                     stage_mul(i // 2 - 3)
             else:
-                if 3 <= i:
-                    stage_max((i - 3) // 2)
-                if 5 <= i:
+                if i >= 3:
+                    stage_nb((i - 3) // 2)
+                if i >= 5:
                     stage_exp((i - 5) // 2, range(4, 8))
             stage_b(i + 1)
 
         stage_d(14)
         stage_q1(15)
-        stage_m1(15)
+        stage_m1(15, False)
         stage_max(6)
-        stage_exp(5, range(4, 8))
-        stage_d(15, last=True)
+        stage_d(15, (nc.scalar.copy, None))
         stage_q2(14)
         stage_m2(7)
+        stage_d(15, (None, nc.vector.tensor_copy))
+        stage_nb(6)
+        stage_exp(5, range(4, 8))
         stage_exp(6, range(8))
-        stage_q2(15, 2)
+        stage_q2(15, (0,))
         stage_m2(8)
-        stage_m2(9)
         stage_max(7)
-        stage_mul(5)
+        stage_q2(15, (1,))
+        stage_m2(9)
+        stage_rc(5)
         stage_max(8)
+        stage_nb(7)
         stage_max(9)
+        stage_nb(8)
+        stage_mul(5)
+        stage_nb(9)
         stage_exp(7, range(4))
-        stage_mul(6)
+        stage_rc(6)
         stage_exp(8, range(2))
         stage_exp(9, range(2))
-        stage_mul(7)
+        stage_rc(7)
+        stage_mul(6)
+        stage_mul_scalar(7)
+        stage_rc(8)
+        stage_rc(9)
         stage_mul(8)
         stage_mul(9)

@@ -17,15 +17,16 @@ AXIS_X = mybir.AxisListType.X
 COPY = mybir.ActivationFunctionType.Copy
 EXP = mybir.ActivationFunctionType.Exp
 
-B, S, D, N, F = 64, 64, 512, 128, 512
 P = 128
-FLOPS = 2 * B * S * D * F + 2 * N * F * F + 2 * B * N * S * F
+PACK = 4
+SAMPLES, SLOTS, FEATURES, OBJECTS = 64, 64, 512, 128
+FLOPS = 2 * SAMPLES * SLOTS * FEATURES**2 + 2 * OBJECTS * FEATURES**2 + 2 * SAMPLES * OBJECTS * SLOTS * FEATURES
+LOGIT_SCALE = float(FEATURES) ** -0.5
 
-ROWS = B * S
-PAIRS = ROWS // (2 * P)
-CHUNKS = PAIRS // 2
-CB = 512 // S
-LOGIT_SCALE = float(D) ** -0.5
+PAIRS = SAMPLES * SLOTS // (2 * P)
+LAST = PAIRS - 1
+UNITS = [(4 * u, 4) for u in range(7)] + [(28, 2), (30, 1), (31, 1)]
+Q, K = 0, 1
 
 
 def tile_actionbindingattention_pb_w4_kernel(
@@ -33,364 +34,359 @@ def tile_actionbindingattention_pb_w4_kernel(
 ):
     nc = tc.nc
     with ExitStack() as ctx:
-        const = ctx.enter_context(tc.tile_pool(name="const", bufs=1))
+        keep = ctx.enter_context(tc.tile_pool(name="keep", bufs=1))
         work = ctx.enter_context(tc.tile_pool(name="work", bufs=4))
-        outs = ctx.enter_context(tc.tile_pool(name="outs", bufs=11))
-        psx = ctx.enter_context(tc.psum_pool(name="psx", bufs=2))
-        psq = ctx.enter_context(tc.psum_pool(name="psq", bufs=4))
-        psl = ctx.enter_context(tc.psum_pool(name="psl", bufs=2))
+        soft = ctx.enter_context(tc.tile_pool(name="soft", bufs=len(UNITS)))
+        turn_psum = ctx.enter_context(tc.psum_pool(name="turn_psum", bufs=2))
+        proj_psum = ctx.enter_context(tc.psum_pool(name="proj_psum", bufs=4))
+        logit_psum = ctx.enter_context(tc.psum_pool(name="logit_psum", bufs=2))
         ctx.enter_context(tc.manual_schedule())
 
-        xb = []
-        rows_flat = slots_bytes.rearrange("b s k -> (b s) k")
+        scale4 = keep.tile([P, PACK], F32, name="scale4")
+        nc.scalar.dma_start(out=scale4[:], in_=slots_scale.rearrange("a b (p t) -> p (a b t)", t=PACK))
+        ident_rows = keep.tile([P, FEATURES], BF16, name="ident_rows", align_bytes=64)
+        nc.scalar.dma_start(out=ident_rows[:], in_=ident)
 
-        def load_x(first, count):
-            t = const.tile([P, 2 * count, D], U8, name="xb%d" % first, align_bytes=64)
-            src = rows_flat[first * 2 * P : (first + count) * 2 * P, :]
-            nc.sync.dma_start(out=t[:], in_=src.rearrange("(j p) k -> p j k", p=P))
-            for i in range(count):
-                xb.append(t[:, 2 * i : 2 * i + 2, :])
-
-        s4 = const.tile([P, 4], F32, name="s4")
-        nc.scalar.dma_start(out=s4[:], in_=slots_scale.rearrange("a b (p t) -> p (a b t)", t=4))
-        s_bc = const.tile([P, 2, D], F32, name="s_bc", align_bytes=64)
-        idb = const.tile([P, F], BF16, name="idb", align_bytes=64)
-        nc.scalar.dma_start(out=idb[:], in_=ident)
-        warm = const.tile([P, 1], F32, name="warm")
+        warm = keep.tile([P, 1], F32, name="warm")
         nc.vector.memset(warm[:], 0.0)
         nc.scalar.activation(out=warm[:], in_=warm[:], func=EXP)
+        eye = keep.tile([P, P], F32, name="eye", align_bytes=64)
+        make_identity(nc, eye[:])
 
-        identf = const.tile([P, P], F32, name="identf", align_bytes=64)
-        make_identity(nc, identf[:])
-        ws_raw = const.tile([P, 2, F], U8, name="ws_raw", align_bytes=64)
-        nc.vector.memset(ws_raw[:].rearrange("p w n -> p (w n)").bitcast(I32), 0)
-        ww_raw = const.tile([P, 2, 2 * F], U8, name="ww_raw", align_bytes=64)
-        ww = const.tile([P, 2, 2 * F], U8, name="ww", align_bytes=64)
-        ws = const.tile([P, 2, F], U8, name="ws", align_bytes=64)
+        raw_bytes = []
+        rows = slots_bytes.rearrange("b s k -> (b s) k")
 
-        def load_w(w, words, scales):
-            nc.sync.dma_start(out=ww_raw[:, w, :].bitcast(I32), in_=words[0].bitcast(I32))
-            for q in range(4):
+        def load_slots(first, pairs):
+            t = keep.tile([P, 2 * pairs, FEATURES], U8, name="slots_%d" % first, align_bytes=64)
+            src = rows[first * 2 * P : (first + pairs) * 2 * P, :]
+            nc.sync.dma_start(out=t[:], in_=src.rearrange("(j p) k -> p j k", p=P))
+            for i in range(pairs):
+                raw_bytes.append(t[:, 2 * i : 2 * i + 2, :])
+
+        words_in = keep.tile([P, 2, 2 * FEATURES], U8, name="words_in", align_bytes=64)
+        scales_in = keep.tile([P, 2, FEATURES], U8, name="scales_in", align_bytes=64)
+        words = keep.tile([P, 2, 2 * FEATURES], U8, name="words", align_bytes=64)
+        scales = keep.tile([P, 2, FEATURES], U8, name="scales", align_bytes=64)
+        nc.vector.memset(scales_in[:].rearrange("p w n -> p (w n)").bitcast(I32), 0)
+
+        def load_weight(w, w_words, w_scales):
+            nc.sync.dma_start(out=words_in[:, w, :].bitcast(I32), in_=w_words[0].bitcast(I32))
+            for b in range(4):
                 nc.sync.dma_start(
-                    out=ws_raw[32 * q : 32 * q + 4, w, :].bitcast(I32),
-                    in_=scales[0, 4 * q : 4 * q + 4, :].bitcast(I32),
+                    out=scales_in[32 * b : 32 * b + 4, w, :].bitcast(I32),
+                    in_=w_scales[0, 4 * b : 4 * b + 4, :].bitcast(I32),
                 )
 
-        def permute_words(eng, w):
-            eng.tensor_copy(
-                out=ww[:, w, :].bitcast(I32).rearrange("p (t g e) -> p t g e", t=4, e=2),
-                in_=ww_raw[:, w, :].bitcast(I32).rearrange("p (g t e) -> p t g e", t=4, e=2),
-            )
-
-        def permute_scales(eng, w):
-            eng.tensor_copy(
-                out=ws[:, w, :].bitcast(I32).rearrange("p (t g) -> p t g", t=4),
-                in_=ws_raw[:, w, :].bitcast(I32).rearrange("p (g t) -> p t g", t=4),
-            )
-
-        load_x(0, 1)
-        load_w(0, Wq_words, Wq_scales)
-        load_x(1, 1)
-        load_w(1, Wk_words, Wk_scales)
+        load_slots(0, 1)
+        load_weight(Q, Wq_words, Wq_scales)
+        load_slots(1, 1)
+        load_weight(K, Wk_words, Wk_scales)
         for first in range(2, PAIRS, 2):
-            load_x(first, 2)
+            load_slots(first, 2)
 
-        xs, xt, xg, xq, qp, qg, qq, lg = {}, {}, {}, {}, {}, {}, {}, {}
-        top, nb, ex, sm, rcp = {}, {}, {}, {}, {}
-        units = [(4 * c, 4) for c in range(CHUNKS - 1)] + [(28, 2), (30, 1), (31, 1)]
+        def permute_words(w):
+            nc.vector.tensor_copy(
+                out=words[:, w, :].bitcast(I32).rearrange("p (t g e) -> p t g e", t=PACK, e=2),
+                in_=words_in[:, w, :].bitcast(I32).rearrange("p (g t e) -> p t g e", t=PACK, e=2),
+            )
 
-        def stage_a(i):
-            t = work.tile([P, 2, D], BF16, name="xs", align_bytes=64)
+        def permute_scales(w):
+            nc.vector.tensor_copy(
+                out=scales[:, w, :].bitcast(I32).rearrange("p (t g) -> p t g", t=PACK),
+                in_=scales_in[:, w, :].bitcast(I32).rearrange("p (g t) -> p t g", t=PACK),
+            )
+
+        scaled, turned, slots4, slots_q, proj, query4, query_q = {}, {}, {}, {}, {}, {}, {}
+        logits, tops, biases, exps, sums, inverses = {}, {}, {}, {}, {}, {}
+
+        scale_rows = keep.tile([P, 2, FEATURES], F32, name="scale_rows", align_bytes=64)
+
+        def scale_slots(i, tiles=(0, 1)):
+            if i not in scaled:
+                scaled[i] = work.tile([P, 2, FEATURES], BF16, name="scaled", align_bytes=64)
             if i < 2:
-                for j in range(2):
+                for j in tiles:
                     nc.vector.tensor_tensor(
-                        out=t[:, j, :], in0=xb[i][:, j, :].bitcast(FP8), in1=s_bc[:, 0, :], op=MULT
+                        out=scaled[i][:, j, :],
+                        in0=raw_bytes[i][:, j, :].bitcast(FP8),
+                        in1=scale_rows[:, 0, :],
+                        op=MULT,
                     )
             else:
                 nc.vector.tensor_tensor(
-                    out=t[:].rearrange("p j k -> p (j k)"),
-                    in0=xb[i].rearrange("p j k -> p (j k)").bitcast(FP8),
-                    in1=s_bc[:].rearrange("p j k -> p (j k)"),
+                    out=scaled[i][:].rearrange("p j k -> p (j k)"),
+                    in0=raw_bytes[i].rearrange("p j k -> p (j k)").bitcast(FP8),
+                    in1=scale_rows[:].rearrange("p j k -> p (j k)"),
                     op=MULT,
                 )
-            xs[i] = t
 
-        def transposes(src, dst):
-            words = src.bitcast(F32)
+        def turn_rows(dst, src):
+            src_words = src.bitcast(F32)
             for u in range(2):
-                nc.tensor.transpose(dst[:, u, :], words[:, u::2], identf[:])
+                nc.tensor.transpose(dst[:, u, :], src_words[:, u::2], eye[:])
 
-        def stage_t(i):
-            t = psx.tile([P, 2, 2, P], F32, name="xt")
+        def lay_rows(dst, src):
+            nc.scalar.copy(
+                out=dst.rearrange("p r t -> p (r t)").bitcast(F32).rearrange("p (r u) -> p r u", u=2),
+                in_=src.rearrange("p u r -> p r u"),
+            )
+
+        def turn_slots(i):
+            turned[i] = turn_psum.tile([P, 2, 2, P], F32, name="turned")
             for j in range(2):
-                transposes(xs[i][:, j, :], t[:, j])
-            xt[i] = t
+                turn_rows(turned[i][:, j], scaled[i][:, j, :])
 
-        def head_pair():
-            t = work.tile([P, 2, P, 4], BF16, name="xg", align_bytes=64)
+        def lay_slots(i):
+            slots4[i] = work.tile([P, 2, P, PACK], BF16, name="slots4", align_bytes=64)
+            nc.scalar.copy(
+                out=slots4[i][:]
+                .rearrange("p j r t -> p j (r t)")
+                .bitcast(F32)
+                .rearrange("p j (r u) -> p j r u", u=2),
+                in_=turned[i][:].rearrange("p j u r -> p j r u"),
+            )
+
+        def turn_and_lay_first_pair():
+            slots4[0] = work.tile([P, 2, P, PACK], BF16, name="slots4", align_bytes=64)
             for j in range(2):
-                h = psx.tile([P, 2, P], F32, name="xt")
-                transposes(xs[0][:, j, :], h)
-                nc.scalar.copy(
-                    out=t[:, j].rearrange("p r t -> p (r t)").bitcast(F32).rearrange("p (r u) -> p r u", u=2),
-                    in_=h[:].rearrange("p u r -> p r u"),
-                )
-            xg[0] = t
+                bank = turn_psum.tile([P, 2, P], F32, name="turned")
+                turn_rows(bank, scaled[0][:, j, :])
+                lay_rows(slots4[0][:, j], bank[:])
 
-        def stage_b(i, parts=1):
-            t = work.tile([P, 2, P, 4], BF16, name="xg", align_bytes=64)
-            n = 2 // parts
-            for h in range(parts):
-                js = slice(n * h, n * h + n)
-                nc.scalar.copy(
-                    out=t[:, js].rearrange("p j r t -> p j (r t)").bitcast(F32).rearrange("p j (r u) -> p j r u", u=2),
-                    in_=xt[i][:, js].rearrange("p j u r -> p j r u"),
+        def quantize_slots(i, lo=0, hi=2):
+            if i not in slots_q:
+                slots_q[i] = (
+                    work.tile([P, 2 * P], U32, name="slot_codes", align_bytes=64),
+                    work.tile([P, 2 * P], U8, name="slot_scales", align_bytes=64),
                 )
-            xg[i] = t
+            codes, code_scales = slots_q[i]
+            cols = slice(P * lo, P * hi)
+            nc.vector.quantize_mx(
+                out=codes[:, cols].bitcast(FP8X4),
+                scales=code_scales[:, cols],
+                in_=slots4[i][:, lo:hi].rearrange("p j r t -> p (j r t)"),
+            )
 
-        def stage_q1(i, parts=1):
-            c = work.tile([P, 2 * P], U32, name="xq", align_bytes=64)
-            s = work.tile([P, 2 * P], U8, name="xqs", align_bytes=64)
-            n = 2 // parts
-            for h in range(parts):
-                cols = slice(P * n * h, P * n * (h + 1))
-                nc.vector.quantize_mx(
-                    out=c[:, cols].bitcast(FP8X4),
-                    scales=s[:, cols],
-                    in_=xg[i][:, n * h : n * h + n].rearrange("p j r t -> p (j r t)"),
-                )
-            xq[i] = (c, s)
-
-        def project(w, codes, scales, fill=False):
-            t = psq.tile([P, 4, P], F32, name="qp")
+        def project(w, codes, code_scales, fill=False):
+            bank = proj_psum.tile([P, PACK, P], F32, name="proj")
             if fill:
                 nc.tensor.matmul(
-                    t[:].rearrange("p t r -> p (t r)"), lhsT=idb[:, :P], rhs=idb[:], start=True, stop=True
-                )
-            for f in range(4):
-                nc.tensor.matmul_mx(
-                    out=t[:, f, :],
-                    lhsT=ww[:, w, 2 * P * f : 2 * P * (f + 1)].bitcast(FP4X4),
-                    lhsT_scale=ws[:, w, P * f : P * (f + 1)],
-                    rhs=codes.bitcast(FP8X4),
-                    rhs_scale=scales,
+                    bank[:].rearrange("p t r -> p (t r)"),
+                    lhsT=ident_rows[:, :P],
+                    rhs=ident_rows[:],
                     start=True,
                     stop=True,
                 )
-            return t
+            for t in range(PACK):
+                nc.tensor.matmul_mx(
+                    out=bank[:, t, :],
+                    lhsT=words[:, w, 2 * P * t : 2 * P * (t + 1)].bitcast(FP4X4),
+                    lhsT_scale=scales[:, w, P * t : P * (t + 1)],
+                    rhs=codes.bitcast(FP8X4),
+                    rhs_scale=code_scales,
+                    start=True,
+                    stop=True,
+                )
+            return bank
 
-        def stage_m1(i, fill=True):
-            c, s = xq[i]
-            qp[i] = [project(0, c[:, P * j : P * (j + 1)], s[:, P * j : P * (j + 1)], fill and j == 0) for j in range(2)]
+        def queries(i, tiles=(0, 1), fill=True):
+            codes, code_scales = slots_q[i]
+            for j in tiles:
+                cols = slice(P * j, P * (j + 1))
+                proj[i, j] = project(Q, codes[:, cols], code_scales[:, cols], fill and j == 0)
 
-        def stage_d(i, copies=(nc.scalar.copy, nc.scalar.copy)):
-            if i not in qg:
-                qg[i] = work.tile([P, 2, P, 4], BF16, name="qg", align_bytes=64)
-            for j in range(2):
-                if copies[j]:
-                    copies[j](out=qg[i][:, j], in_=qp[i][j][:].rearrange("p t r -> p r t"))
+        def lay_query(i, j, copy):
+            if i not in query4:
+                query4[i] = work.tile([P, 2, P, PACK], BF16, name="query4", align_bytes=64)
+            copy(out=query4[i][:, j], in_=proj[i, j][:].rearrange("p t r -> p r t"))
 
-        def stage_q2(i, tiles=None):
-            h = i % 2
-            if i // 2 not in qq:
-                c = work.tile([P, 4 * P], U32, name="qq", align_bytes=64)
-                s = work.tile([P, 4 * P], U8, name="qqs", align_bytes=64)
-                qq[i // 2] = (c, s)
-            c, s = qq[i // 2]
-            lo, hi = (tiles[0], tiles[0] + 1) if tiles else (0, 2)
-            cols = slice(P * (2 * h + lo), P * (2 * h + hi))
+        def quantize_queries(i, lo=0, hi=2):
+            if i // 2 not in query_q:
+                query_q[i // 2] = (
+                    work.tile([P, 4 * P], U32, name="query_codes", align_bytes=64),
+                    work.tile([P, 4 * P], U8, name="query_scales", align_bytes=64),
+                )
+            codes, code_scales = query_q[i // 2]
+            first = 2 * (i % 2)
+            cols = slice(P * (first + lo), P * (first + hi))
             nc.vector.quantize_mx(
-                out=c[:, cols].bitcast(FP8X4),
-                scales=s[:, cols],
-                in_=qg[i][:, lo:hi].rearrange("p j r t -> p (j r t)"),
+                out=codes[:, cols].bitcast(FP8X4),
+                scales=code_scales[:, cols],
+                in_=query4[i][:, lo:hi].rearrange("p j r t -> p (j r t)"),
             )
 
-        def stage_m2(c):
-            first, tiles = units[c]
-            if c in (7, 8):
-                t = psx.tile([P, 2 * tiles, S], F32, name="xt")
-            else:
-                t = psl.tile([P, 2 * tiles, S], F32, name="lg")
-            codes, scales = qq[first // 4]
+        def multiply_keys(u, pool=logit_psum, name="logits"):
+            first, tiles = UNITS[u]
+            logits[u] = pool.tile([P, 2 * tiles, SLOTS], F32, name=name)
+            codes, code_scales = query_q[first // 4]
             cols = slice(P * (first % 4), P * (first % 4 + tiles))
             nc.tensor.matmul_mx(
-                out=t[:].rearrange("p b s -> p (b s)"),
-                lhsT=kq[:].bitcast(FP8X4),
-                lhsT_scale=kqs[:],
+                out=logits[u][:].rearrange("p b s -> p (b s)"),
+                lhsT=key_codes[:].bitcast(FP8X4),
+                lhsT_scale=key_scales[:],
                 rhs=codes[:, cols].bitcast(FP8X4),
-                rhs_scale=scales[:, cols],
+                rhs_scale=code_scales[:, cols],
                 start=True,
                 stop=True,
             )
-            lg[c] = t
 
-        def stage_max(c):
-            samples = 2 * units[c][1]
-            mx = outs.tile([P, samples], F32, name="mx")
-            nc.vector.tensor_reduce(out=mx[:], in_=lg[c][:], axis=AXIS_X, op=MAX)
-            top[c] = mx
+        def find_tops(u):
+            tops[u] = soft.tile([P, 2 * UNITS[u][1]], F32, name="tops")
+            nc.vector.tensor_reduce(out=tops[u][:], in_=logits[u][:], axis=AXIS_X, op=MAX)
 
-        def stage_nb(c):
-            samples = 2 * units[c][1]
-            t = outs.tile([P, samples], F32, name="nb")
-            nc.vector.tensor_scalar(out=t[:], in0=top[c][:], scalar1=-LOGIT_SCALE, scalar2=None, op0=MULT)
-            nb[c] = t
-            ex[c] = outs.tile([P, samples, S], F32, name="ex")
-            sm[c] = outs.tile([P, samples], F32, name="sm")
+        def negate_tops(u, on_scalar):
+            biases[u] = soft.tile([P, 2 * UNITS[u][1]], F32, name="biases")
+            if on_scalar:
+                nc.scalar.activation(out=biases[u][:], in_=tops[u][:], func=COPY, scale=-LOGIT_SCALE)
+            else:
+                nc.vector.tensor_scalar(
+                    out=biases[u][:], in0=tops[u][:], scalar1=-LOGIT_SCALE, scalar2=None, op0=MULT
+                )
 
-        def stage_exp(c, samples):
+        def exponentiate(u, samples):
+            if u not in exps:
+                exps[u] = soft.tile([P, 2 * UNITS[u][1], SLOTS], F32, name="exps")
+                sums[u] = soft.tile([P, 2 * UNITS[u][1]], F32, name="sums")
             for b in samples:
                 nc.scalar.activation(
-                    out=ex[c][:, b, :],
-                    in_=lg[c][:, b, :],
+                    out=exps[u][:, b, :],
+                    in_=logits[u][:, b, :],
                     func=EXP,
-                    bias=nb[c][:, b : b + 1],
+                    bias=biases[u][:, b : b + 1],
                     scale=LOGIT_SCALE,
-                    accum_out=sm[c][:, b : b + 1],
+                    accum_out=sums[u][:, b : b + 1],
                 )
 
-        def stage_rc(c):
-            rcp[c] = outs.tile([P, 2 * units[c][1]], F32, name="rc")
-            nc.vector.reciprocal(out=rcp[c][:], in_=sm[c][:])
+        def invert_sums(u):
+            inverses[u] = soft.tile([P, 2 * UNITS[u][1]], F32, name="inverses")
+            nc.vector.reciprocal(out=inverses[u][:], in_=sums[u][:])
 
-        def stage_mul(c):
-            first, tiles = units[c]
+        def divide_and_store(u, on_scalar=False):
+            first, tiles = UNITS[u]
             samples = 2 * tiles
-            rc = rcp[c]
-            o = outs.tile([P, samples, S], F32, name="o")
-            nc.vector.tensor_tensor(
-                out=o[:], in0=ex[c][:], in1=rc[:].unsqueeze(2).to_broadcast([P, samples, S]), op=MULT
-            )
-            nc.sync.dma_start(
-                out=out[2 * first : 2 * first + samples].rearrange("b n s -> n b s"), in_=o[:]
-            )
-
-        def stage_mul_gpsimd(c):
-            first, tiles = units[c]
-            samples = 2 * tiles
-            o = outs.tile([P, samples, S], F32, name="o")
-            nc.gpsimd.tensor_tensor(
-                out=o[:], in0=ex[c][:], in1=rcp[c][:].unsqueeze(2).to_broadcast([P, samples, S]), op=MULT
-            )
-            nc.sync.dma_start(
-                out=out[2 * first : 2 * first + samples].rearrange("b n s -> n b s"), in_=o[:]
-            )
-
-        def stage_mul_scalar(c):
-            first, tiles = units[c]
-            samples = 2 * tiles
-            o = outs.tile([P, samples, S], F32, name="o")
-            for b in range(samples):
-                nc.scalar.activation(
-                    out=o[:, b, :], in_=ex[c][:, b, :], func=COPY, scale=rcp[c][:, b : b + 1]
+            shares = soft.tile([P, samples, SLOTS], F32, name="shares")
+            if on_scalar:
+                for b in range(samples):
+                    nc.scalar.activation(
+                        out=shares[:, b, :], in_=exps[u][:, b, :], func=COPY, scale=inverses[u][:, b : b + 1]
+                    )
+            else:
+                nc.vector.tensor_tensor(
+                    out=shares[:],
+                    in0=exps[u][:],
+                    in1=inverses[u][:].unsqueeze(2).to_broadcast([P, samples, SLOTS]),
+                    op=MULT,
                 )
             nc.sync.dma_start(
-                out=out[2 * first : 2 * first + samples].rearrange("b n s -> n b s"), in_=o[:]
+                out=out[2 * first : 2 * first + samples].rearrange("b n s -> n b s"), in_=shares[:]
             )
 
-        ig = const.tile([P, P, 4], BF16, name="ig", align_bytes=64)
-        iq = const.tile([P, P], U32, name="iq", align_bytes=64)
-        iqs = const.tile([P, P], U8, name="iqs", align_bytes=64)
-        kg = const.tile([P, P, 4], BF16, name="kg", align_bytes=64)
-        kq = const.tile([P, P], U32, name="kq", align_bytes=64)
-        kqs = const.tile([P, P], U8, name="kqs", align_bytes=64)
-        sp = psl.tile([P, 4, P], F32, name="lg")
-        for t in range(4):
-            nc.tensor.transpose(sp[:, t, :], s4[:, t : t + 1].to_broadcast([P, P]), identf[:])
+        scale_bank = logit_psum.tile([P, PACK, P], F32, name="logits")
+        for t in range(PACK):
+            nc.tensor.transpose(scale_bank[:, t, :], scale4[:, t : t + 1].to_broadcast([P, P]), eye[:])
         for j in range(2):
             nc.scalar.copy(
-                out=s_bc[:, j, :].rearrange("p (n t) -> p n t", t=4), in_=sp[:].rearrange("p t n -> p n t")
+                out=scale_rows[:, j, :].rearrange("p (n t) -> p n t", t=PACK),
+                in_=scale_bank[:].rearrange("p t n -> p n t"),
             )
-        it = psl.tile([P, 2, P], F32, name="lg")
-        transposes(idb[:], it)
-        nc.scalar.copy(
-            out=ig[:].rearrange("p r t -> p (r t)").bitcast(F32).rearrange("p (r u) -> p r u", u=2),
-            in_=it[:].rearrange("p u r -> p r u"),
+        ident4 = keep.tile([P, P, PACK], BF16, name="ident4", align_bytes=64)
+        ident_bank = logit_psum.tile([P, 2, P], F32, name="logits")
+        turn_rows(ident_bank, ident_rows[:])
+        lay_rows(ident4[:], ident_bank[:])
+
+        permute_words(Q)
+        scale_slots(0)
+        turn_and_lay_first_pair()
+        permute_scales(Q)
+        scale_slots(1, (0,))
+        quantize_slots(0, 0, 1)
+        queries(0, (0,))
+        scale_slots(1, (1,))
+        quantize_slots(0, 1, 2)
+        queries(0, (1,))
+        turn_slots(1)
+
+        permute_words(K)
+        permute_scales(K)
+        ident_codes = keep.tile([P, P], U32, name="ident_codes", align_bytes=64)
+        ident_scales = keep.tile([P, P], U8, name="ident_scales", align_bytes=64)
+        nc.vector.quantize_mx(
+            out=ident_codes[:].bitcast(FP8X4), scales=ident_scales[:], in_=ident4[:].rearrange("p r t -> p (r t)")
         )
-        stage_a(0)
-        head_pair()
-        permute_words(nc.vector, 0)
-        permute_scales(nc.vector, 0)
-        stage_q1(0, 2)
-        stage_m1(0)
-        stage_a(1)
-        stage_t(1)
-        permute_words(nc.vector, 1)
-        permute_scales(nc.vector, 1)
-        nc.vector.quantize_mx(out=iq[:].bitcast(FP8X4), scales=iqs[:], in_=ig[:].rearrange("p r t -> p (r t)"))
-        stage_d(0)
-        stage_b(1)
-        stage_a(2)
+        key_bank = project(K, ident_codes[:], ident_scales[:])
+        for j in range(2):
+            lay_query(0, j, nc.scalar.copy)
+        lay_slots(1)
+        scale_slots(2)
+        key4 = keep.tile([P, P, PACK], BF16, name="key4", align_bytes=64)
+        nc.scalar.copy(out=key4[:], in_=key_bank[:].rearrange("p t r -> p r t"))
+        key_codes = keep.tile([P, P], U32, name="key_codes", align_bytes=64)
+        key_scales = keep.tile([P, P], U8, name="key_scales", align_bytes=64)
 
-        for i in range(1, PAIRS - 1):
-            if i % 2 == 0 and i >= 6:
-                stage_rc(i // 2 - 3)
-            if i + 2 < PAIRS:
-                stage_a(i + 2)
-            stage_t(i + 1)
-            if i == PAIRS - 2:
-                stage_d(i - 1, (nc.scalar.copy, None))
-            elif i > 1:
-                stage_d(i - 1)
-            if i == 2:
-                nc.scalar.copy(out=kg[:], in_=kp[:].rearrange("p t r -> p r t"))
-            stage_q1(i)
-            stage_m1(i)
+        for i in range(1, LAST):
+            u = i // 2
+            even = i % 2 == 0
+            if even and u >= 3:
+                invert_sums(u - 3)
+            if i + 2 <= LAST:
+                scale_slots(i + 2)
+            turn_slots(i + 1)
+            if even and u >= 2:
+                negate_tops(u - 2, on_scalar=True)
+            if i > 1:
+                lay_query(i - 1, 0, nc.scalar.copy)
+                lay_query(i - 1, 1, nc.scalar.copy if i + 2 <= LAST else nc.vector.tensor_copy)
+            quantize_slots(i)
+            queries(i)
+            if not even and u >= 1:
+                find_tops(u - 1)
+            quantize_queries(i - 1)
             if i == 1:
-                kp = project(1, iq[:], iqs[:])
-            if i == PAIRS - 2:
-                stage_d(i - 1, (None, nc.vector.tensor_copy))
-            if i % 2 == 1 and i >= 3:
-                stage_max((i - 3) // 2)
-            stage_q2(i - 1)
-            if i == 2:
                 nc.vector.quantize_mx(
-                    out=kq[:].bitcast(FP8X4), scales=kqs[:], in_=kg[:].rearrange("p r t -> p (r t)")
+                    out=key_codes[:].bitcast(FP8X4), scales=key_scales[:], in_=key4[:].rearrange("p r t -> p (r t)")
                 )
-            if i % 2 == 0:
-                stage_m2(i // 2 - 1)
-                if i >= 4:
-                    stage_exp(i // 2 - 2, range(4))
-                if i >= 6:
-                    stage_mul(i // 2 - 3)
-            else:
-                if i >= 3:
-                    stage_nb((i - 3) // 2)
-                if i >= 5:
-                    stage_exp((i - 5) // 2, range(4, 8))
-            stage_b(i + 1)
+            if even:
+                multiply_keys(u - 1)
+                if u >= 2:
+                    exponentiate(u - 2, range(0, 4))
+                if u >= 3:
+                    divide_and_store(u - 3)
+            elif u >= 2:
+                exponentiate(u - 2, range(4, 8))
+            lay_slots(i + 1)
 
-        stage_d(14)
-        stage_q1(15)
-        stage_m1(15, False)
-        stage_max(6)
-        stage_d(15, (nc.scalar.copy, None))
-        stage_q2(14)
-        stage_m2(7)
-        stage_d(15, (None, nc.vector.tensor_copy))
-        stage_nb(6)
-        stage_exp(5, range(4, 8))
-        stage_exp(6, range(8))
-        stage_q2(15, (0,))
-        stage_m2(8)
-        stage_max(7)
-        stage_q2(15, (1,))
-        stage_m2(9)
-        stage_rc(5)
-        stage_max(8)
-        stage_nb(7)
-        stage_max(9)
-        stage_nb(8)
-        stage_mul(5)
-        stage_nb(9)
-        stage_exp(7, range(4))
-        stage_rc(6)
-        stage_exp(8, range(2))
-        stage_exp(9, range(2))
-        stage_rc(7)
-        stage_mul(6)
-        stage_mul_scalar(7)
-        stage_rc(8)
-        stage_rc(9)
-        stage_mul(8)
-        stage_mul(9)
+        quantize_slots(15)
+        find_tops(6)
+        queries(15, fill=False)
+        lay_query(14, 0, nc.scalar.copy)
+        lay_query(14, 1, nc.scalar.copy)
+        lay_query(15, 0, nc.scalar.copy)
+        quantize_queries(14)
+        negate_tops(6, on_scalar=False)
+        multiply_keys(7, turn_psum, "turned")
+        lay_query(15, 1, nc.vector.tensor_copy)
+        quantize_queries(15, 0, 1)
+        find_tops(7)
+        exponentiate(5, range(4, 8))
+        quantize_queries(15, 1, 2)
+        invert_sums(5)
+        multiply_keys(8, turn_psum, "turned")
+        multiply_keys(9)
+        find_tops(8)
+        negate_tops(7, on_scalar=False)
+        exponentiate(6, range(8))
+        find_tops(9)
+        negate_tops(8, on_scalar=False)
+        divide_and_store(5)
+        exponentiate(7, range(4))
+        invert_sums(6)
+        exponentiate(8, range(2))
+        negate_tops(9, on_scalar=False)
+        invert_sums(7)
+        invert_sums(8)
+        divide_and_store(7, on_scalar=True)
+        divide_and_store(6)
+        exponentiate(9, range(2))
+        invert_sums(9)
+        divide_and_store(8)
+        divide_and_store(9)

from contextlib import ExitStack

import concourse.mybir as mybir
from concourse.masks import make_identity

F32 = mybir.dt.float32
BF16 = mybir.dt.bfloat16
I32 = mybir.dt.int32
U32 = mybir.dt.uint32
U8 = mybir.dt.uint8
FP8 = mybir.dt.float8_e4m3fn
FP8X4 = mybir.dt.float8_e4m3fn_x4
FP4X4 = mybir.dt.float4_e2m1fn_x4
MULT = mybir.AluOpType.mult
MAX = mybir.AluOpType.max
AXIS_X = mybir.AxisListType.X
COPY = mybir.ActivationFunctionType.Copy
EXP = mybir.ActivationFunctionType.Exp

P = 128
PACK = 4
SAMPLES, SLOTS, FEATURES, OBJECTS = 64, 64, 512, 128
FLOPS = 2 * SAMPLES * SLOTS * FEATURES**2 + 2 * OBJECTS * FEATURES**2 + 2 * SAMPLES * OBJECTS * SLOTS * FEATURES
LOGIT_SCALE = float(FEATURES) ** -0.5

PAIRS = SAMPLES * SLOTS // (2 * P)
LAST = PAIRS - 1
UNITS = [(4 * u, 4) for u in range(7)] + [(28, 2), (30, 1), (31, 1)]
Q, K = 0, 1


def tile_actionbindingattention_pb_w4_kernel(
    tc, slots_bytes, slots_scale, ident, Wq_words, Wq_scales, Wk_words, Wk_scales, out
):
    nc = tc.nc
    with ExitStack() as ctx:
        keep = ctx.enter_context(tc.tile_pool(name="keep", bufs=1))
        work = ctx.enter_context(tc.tile_pool(name="work", bufs=4))
        soft = ctx.enter_context(tc.tile_pool(name="soft", bufs=len(UNITS)))
        turn_psum = ctx.enter_context(tc.psum_pool(name="turn_psum", bufs=2))
        proj_psum = ctx.enter_context(tc.psum_pool(name="proj_psum", bufs=4))
        logit_psum = ctx.enter_context(tc.psum_pool(name="logit_psum", bufs=2))
        ctx.enter_context(tc.manual_schedule())

        scale4 = keep.tile([P, PACK], F32, name="scale4")
        nc.scalar.dma_start(out=scale4[:], in_=slots_scale.rearrange("a b (p t) -> p (a b t)", t=PACK))
        ident_rows = keep.tile([P, FEATURES], BF16, name="ident_rows", align_bytes=64)
        nc.scalar.dma_start(out=ident_rows[:], in_=ident)

        warm = keep.tile([P, 1], F32, name="warm")
        nc.vector.memset(warm[:], 0.0)
        nc.scalar.activation(out=warm[:], in_=warm[:], func=EXP)
        eye = keep.tile([P, P], F32, name="eye", align_bytes=64)
        make_identity(nc, eye[:])

        raw_bytes = []
        rows = slots_bytes.rearrange("b s k -> (b s) k")

        def load_slots(first, pairs):
            t = keep.tile([P, 2 * pairs, FEATURES], U8, name="slots_%d" % first, align_bytes=64)
            src = rows[first * 2 * P : (first + pairs) * 2 * P, :]
            nc.sync.dma_start(out=t[:], in_=src.rearrange("(j p) k -> p j k", p=P))
            for i in range(pairs):
                raw_bytes.append(t[:, 2 * i : 2 * i + 2, :])

        words_in = keep.tile([P, 2, 2 * FEATURES], U8, name="words_in", align_bytes=64)
        scales_in = keep.tile([P, 2, FEATURES], U8, name="scales_in", align_bytes=64)
        words = keep.tile([P, 2, 2 * FEATURES], U8, name="words", align_bytes=64)
        scales = keep.tile([P, 2, FEATURES], U8, name="scales", align_bytes=64)
        nc.vector.memset(scales_in[:].rearrange("p w n -> p (w n)").bitcast(I32), 0)

        def load_weight(w, w_words, w_scales):
            nc.sync.dma_start(out=words_in[:, w, :].bitcast(I32), in_=w_words[0].bitcast(I32))
            for b in range(4):
                nc.sync.dma_start(
                    out=scales_in[32 * b : 32 * b + 4, w, :].bitcast(I32),
                    in_=w_scales[0, 4 * b : 4 * b + 4, :].bitcast(I32),
                )

        load_slots(0, 1)
        load_weight(Q, Wq_words, Wq_scales)
        load_slots(1, 1)
        load_weight(K, Wk_words, Wk_scales)
        for first in range(2, PAIRS, 2):
            load_slots(first, 2)

        def permute_words(w):
            nc.vector.tensor_copy(
                out=words[:, w, :].bitcast(I32).rearrange("p (t g e) -> p t g e", t=PACK, e=2),
                in_=words_in[:, w, :].bitcast(I32).rearrange("p (g t e) -> p t g e", t=PACK, e=2),
            )

        def permute_scales(w):
            nc.vector.tensor_copy(
                out=scales[:, w, :].bitcast(I32).rearrange("p (t g) -> p t g", t=PACK),
                in_=scales_in[:, w, :].bitcast(I32).rearrange("p (g t) -> p t g", t=PACK),
            )

        scaled, turned, slots4, slots_q, proj, query4, query_q = {}, {}, {}, {}, {}, {}, {}
        logits, tops, biases, exps, sums, inverses = {}, {}, {}, {}, {}, {}

        scale_rows = keep.tile([P, 2, FEATURES], F32, name="scale_rows", align_bytes=64)

        def scale_slots(i, tiles=(0, 1)):
            if i not in scaled:
                scaled[i] = work.tile([P, 2, FEATURES], BF16, name="scaled", align_bytes=64)
            if i < 2:
                for j in tiles:
                    nc.vector.tensor_tensor(
                        out=scaled[i][:, j, :],
                        in0=raw_bytes[i][:, j, :].bitcast(FP8),
                        in1=scale_rows[:, 0, :],
                        op=MULT,
                    )
            else:
                nc.vector.tensor_tensor(
                    out=scaled[i][:].rearrange("p j k -> p (j k)"),
                    in0=raw_bytes[i].rearrange("p j k -> p (j k)").bitcast(FP8),
                    in1=scale_rows[:].rearrange("p j k -> p (j k)"),
                    op=MULT,
                )

        def turn_rows(dst, src):
            src_words = src.bitcast(F32)
            for u in range(2):
                nc.tensor.transpose(dst[:, u, :], src_words[:, u::2], eye[:])

        def lay_rows(dst, src):
            nc.scalar.copy(
                out=dst.rearrange("p r t -> p (r t)").bitcast(F32).rearrange("p (r u) -> p r u", u=2),
                in_=src.rearrange("p u r -> p r u"),
            )

        def turn_slots(i):
            turned[i] = turn_psum.tile([P, 2, 2, P], F32, name="turned")
            for j in range(2):
                turn_rows(turned[i][:, j], scaled[i][:, j, :])

        def lay_slots(i):
            slots4[i] = work.tile([P, 2, P, PACK], BF16, name="slots4", align_bytes=64)
            nc.scalar.copy(
                out=slots4[i][:]
                .rearrange("p j r t -> p j (r t)")
                .bitcast(F32)
                .rearrange("p j (r u) -> p j r u", u=2),
                in_=turned[i][:].rearrange("p j u r -> p j r u"),
            )

        def turn_and_lay_first_pair():
            slots4[0] = work.tile([P, 2, P, PACK], BF16, name="slots4", align_bytes=64)
            for j in range(2):
                bank = turn_psum.tile([P, 2, P], F32, name="turned")
                turn_rows(bank, scaled[0][:, j, :])
                lay_rows(slots4[0][:, j], bank[:])

        def quantize_slots(i, lo=0, hi=2):
            if i not in slots_q:
                slots_q[i] = (
                    work.tile([P, 2 * P], U32, name="slot_codes", align_bytes=64),
                    work.tile([P, 2 * P], U8, name="slot_scales", align_bytes=64),
                )
            codes, code_scales = slots_q[i]
            cols = slice(P * lo, P * hi)
            nc.vector.quantize_mx(
                out=codes[:, cols].bitcast(FP8X4),
                scales=code_scales[:, cols],
                in_=slots4[i][:, lo:hi].rearrange("p j r t -> p (j r t)"),
            )

        def project(w, codes, code_scales, fill=False):
            bank = proj_psum.tile([P, PACK, P], F32, name="proj")
            if fill:
                nc.tensor.matmul(
                    bank[:].rearrange("p t r -> p (t r)"),
                    lhsT=ident_rows[:, :P],
                    rhs=ident_rows[:],
                    start=True,
                    stop=True,
                )
            for t in range(PACK):
                nc.tensor.matmul_mx(
                    out=bank[:, t, :],
                    lhsT=words[:, w, 2 * P * t : 2 * P * (t + 1)].bitcast(FP4X4),
                    lhsT_scale=scales[:, w, P * t : P * (t + 1)],
                    rhs=codes.bitcast(FP8X4),
                    rhs_scale=code_scales,
                    start=True,
                    stop=True,
                )
            return bank

        def queries(i, tiles=(0, 1), fill=True):
            codes, code_scales = slots_q[i]
            for j in tiles:
                cols = slice(P * j, P * (j + 1))
                proj[i, j] = project(Q, codes[:, cols], code_scales[:, cols], fill and j == 0)

        def lay_query(i, j, copy):
            if i not in query4:
                query4[i] = work.tile([P, 2, P, PACK], BF16, name="query4", align_bytes=64)
            copy(out=query4[i][:, j], in_=proj[i, j][:].rearrange("p t r -> p r t"))

        def quantize_queries(i, lo=0, hi=2):
            if i // 2 not in query_q:
                query_q[i // 2] = (
                    work.tile([P, 4 * P], U32, name="query_codes", align_bytes=64),
                    work.tile([P, 4 * P], U8, name="query_scales", align_bytes=64),
                )
            codes, code_scales = query_q[i // 2]
            first = 2 * (i % 2)
            cols = slice(P * (first + lo), P * (first + hi))
            nc.vector.quantize_mx(
                out=codes[:, cols].bitcast(FP8X4),
                scales=code_scales[:, cols],
                in_=query4[i][:, lo:hi].rearrange("p j r t -> p (j r t)"),
            )

        def multiply_keys(u, pool=logit_psum, name="logits"):
            first, tiles = UNITS[u]
            logits[u] = pool.tile([P, 2 * tiles, SLOTS], F32, name=name)
            codes, code_scales = query_q[first // 4]
            cols = slice(P * (first % 4), P * (first % 4 + tiles))
            nc.tensor.matmul_mx(
                out=logits[u][:].rearrange("p b s -> p (b s)"),
                lhsT=key_codes[:].bitcast(FP8X4),
                lhsT_scale=key_scales[:],
                rhs=codes[:, cols].bitcast(FP8X4),
                rhs_scale=code_scales[:, cols],
                start=True,
                stop=True,
            )

        def find_tops(u):
            tops[u] = soft.tile([P, 2 * UNITS[u][1]], F32, name="tops")
            nc.vector.tensor_reduce(out=tops[u][:], in_=logits[u][:], axis=AXIS_X, op=MAX)

        def negate_tops(u, on_scalar):
            biases[u] = soft.tile([P, 2 * UNITS[u][1]], F32, name="biases")
            if on_scalar:
                nc.scalar.activation(out=biases[u][:], in_=tops[u][:], func=COPY, scale=-LOGIT_SCALE)
            else:
                nc.vector.tensor_scalar(
                    out=biases[u][:], in0=tops[u][:], scalar1=-LOGIT_SCALE, scalar2=None, op0=MULT
                )

        def exponentiate(u, samples):
            if u not in exps:
                exps[u] = soft.tile([P, 2 * UNITS[u][1], SLOTS], F32, name="exps")
                sums[u] = soft.tile([P, 2 * UNITS[u][1]], F32, name="sums")
            for b in samples:
                nc.scalar.activation(
                    out=exps[u][:, b, :],
                    in_=logits[u][:, b, :],
                    func=EXP,
                    bias=biases[u][:, b : b + 1],
                    scale=LOGIT_SCALE,
                    accum_out=sums[u][:, b : b + 1],
                )

        def invert_sums(u):
            inverses[u] = soft.tile([P, 2 * UNITS[u][1]], F32, name="inverses")
            nc.vector.reciprocal(out=inverses[u][:], in_=sums[u][:])

        def divide_and_store(u, on_scalar=False):
            first, tiles = UNITS[u]
            samples = 2 * tiles
            shares = soft.tile([P, samples, SLOTS], F32, name="shares")
            if on_scalar:
                for b in range(samples):
                    nc.scalar.activation(
                        out=shares[:, b, :], in_=exps[u][:, b, :], func=COPY, scale=inverses[u][:, b : b + 1]
                    )
            else:
                nc.vector.tensor_tensor(
                    out=shares[:],
                    in0=exps[u][:],
                    in1=inverses[u][:].unsqueeze(2).to_broadcast([P, samples, SLOTS]),
                    op=MULT,
                )
            nc.sync.dma_start(
                out=out[2 * first : 2 * first + samples].rearrange("b n s -> n b s"), in_=shares[:]
            )

        scale_bank = logit_psum.tile([P, PACK, P], F32, name="logits")
        for t in range(PACK):
            nc.tensor.transpose(scale_bank[:, t, :], scale4[:, t : t + 1].to_broadcast([P, P]), eye[:])
        for j in range(2):
            nc.scalar.copy(
                out=scale_rows[:, j, :].rearrange("p (n t) -> p n t", t=PACK),
                in_=scale_bank[:].rearrange("p t n -> p n t"),
            )
        ident4 = keep.tile([P, P, PACK], BF16, name="ident4", align_bytes=64)
        ident_bank = logit_psum.tile([P, 2, P], F32, name="logits")
        turn_rows(ident_bank, ident_rows[:])
        lay_rows(ident4[:], ident_bank[:])

        permute_words(Q)
        scale_slots(0)
        turn_and_lay_first_pair()
        permute_scales(Q)
        scale_slots(1, (0,))
        quantize_slots(0, 0, 1)
        queries(0, (0,))
        scale_slots(1, (1,))
        quantize_slots(0, 1, 2)
        queries(0, (1,))
        turn_slots(1)

        permute_words(K)
        permute_scales(K)
        ident_codes = keep.tile([P, P], U32, name="ident_codes", align_bytes=64)
        ident_scales = keep.tile([P, P], U8, name="ident_scales", align_bytes=64)
        nc.vector.quantize_mx(
            out=ident_codes[:].bitcast(FP8X4), scales=ident_scales[:], in_=ident4[:].rearrange("p r t -> p (r t)")
        )
        key_bank = project(K, ident_codes[:], ident_scales[:])
        for j in range(2):
            lay_query(0, j, nc.scalar.copy)
        lay_slots(1)
        scale_slots(2)
        key4 = keep.tile([P, P, PACK], BF16, name="key4", align_bytes=64)
        nc.scalar.copy(out=key4[:], in_=key_bank[:].rearrange("p t r -> p r t"))
        key_codes = keep.tile([P, P], U32, name="key_codes", align_bytes=64)
        key_scales = keep.tile([P, P], U8, name="key_scales", align_bytes=64)

        for i in range(1, LAST):
            u = i // 2
            even = i % 2 == 0
            if even and u >= 3:
                invert_sums(u - 3)
            if i + 2 <= LAST:
                scale_slots(i + 2)
            turn_slots(i + 1)
            if even and u >= 2:
                negate_tops(u - 2, on_scalar=True)
            if i > 1:
                lay_query(i - 1, 0, nc.scalar.copy)
                lay_query(i - 1, 1, nc.scalar.copy if i + 2 <= LAST else nc.vector.tensor_copy)
            quantize_slots(i)
            queries(i)
            if not even and u >= 1:
                find_tops(u - 1)
            quantize_queries(i - 1)
            if i == 1:
                nc.vector.quantize_mx(
                    out=key_codes[:].bitcast(FP8X4), scales=key_scales[:], in_=key4[:].rearrange("p r t -> p (r t)")
                )
            if even:
                multiply_keys(u - 1)
                if u >= 2:
                    exponentiate(u - 2, range(0, 4))
                if u >= 3:
                    divide_and_store(u - 3)
            elif u >= 2:
                exponentiate(u - 2, range(4, 8))
            lay_slots(i + 1)

        quantize_slots(15)
        find_tops(6)
        queries(15, fill=False)
        lay_query(14, 0, nc.scalar.copy)
        lay_query(14, 1, nc.scalar.copy)
        lay_query(15, 0, nc.scalar.copy)
        quantize_queries(14)
        negate_tops(6, on_scalar=False)
        multiply_keys(7, turn_psum, "turned")
        lay_query(15, 1, nc.vector.tensor_copy)
        quantize_queries(15, 0, 1)
        find_tops(7)
        exponentiate(5, range(4, 8))
        quantize_queries(15, 1, 2)
        invert_sums(5)
        multiply_keys(8, turn_psum, "turned")
        multiply_keys(9)
        find_tops(8)
        negate_tops(7, on_scalar=False)
        exponentiate(6, range(8))
        find_tops(9)
        negate_tops(8, on_scalar=False)
        divide_and_store(5)
        exponentiate(7, range(4))
        invert_sums(6)
        exponentiate(8, range(2))
        negate_tops(9, on_scalar=False)
        invert_sums(7)
        invert_sums(8)
        divide_and_store(7, on_scalar=True)
        divide_and_store(6)
        exponentiate(9, range(2))
        invert_sums(9)
        divide_and_store(8)
        divide_and_store(9)
